import numpy as np
import ml_dtypes


def mxq(x, axis, fmt="e4m3"):
    dtype, down = {"e4m3": (ml_dtypes.float8_e4m3fn, 7), "e5m2": (ml_dtypes.float8_e5m2, 14)}[fmt]
    v = np.moveaxis(np.asarray(x, np.float32).astype(ml_dtypes.bfloat16).astype(np.float64), axis, -1)
    blocks = v.reshape(v.shape[:-1] + (-1, 32))
    amax = np.abs(blocks).max(-1, keepdims=True)
    byte = np.maximum(np.where(amax > 0, np.frexp(amax)[1] - 1 + 127, 0) - down, 1)
    scale = np.exp2(byte - 127.0)
    codes = (blocks / scale).astype(np.float32).astype(dtype).astype(np.float64)
    return np.moveaxis((codes * scale).reshape(v.shape), -1, axis)


WIDE = False


def mx_kscale(k):
    if not WIDE:
        return np.ones(k)
    levels = np.array([10, -10, 5, -5, 0])
    a = np.random.permutation(np.resize(levels, k // 512 * 4)).reshape(k // 512, 4)
    idx = np.arange(k)
    return np.exp2(a[idx // 512, idx % 128 // 32])


BF16 = ml_dtypes.bfloat16


def bf(x):
    return np.asarray(x, np.float32).astype(BF16)


def f64(x):
    return np.asarray(x).astype(np.float64)


BS, CIN, H, D, L, P, OUT_DIM = 5, 256, 256, 512, 10, 2, 128
K0, K1 = CIN * P, H * P


def patch_conv_relu(y, w):
    bs, cin, d = y.shape
    out, p = w.shape[0], w.shape[-1]
    q = d // p
    rows = y.reshape(bs, cin, q, p).transpose(0, 2, 1, 3).reshape(bs * q, cin * p)
    wm = w.reshape(out, cin * p).T
    z = (mxq(rows, 1, "e4m3") @ mxq(wm, 0, "e4m3")) * (1.0 / np.sqrt(cin))
    return np.maximum(z, 0.0).reshape(bs, q, out).transpose(0, 2, 1)


def setup_inputs():
    s = mx_kscale(K0).reshape(CIN, P)
    t = mx_kscale(K1)[::P]
    return {"x": bf(np.random.standard_normal((BS, CIN, D)) * np.tile(s, (1, D // P))),
            "w0": bf(np.random.standard_normal((H, CIN, P)) / s * t[:, None, None]),
            "w1": bf(np.random.standard_normal((H, H, P)) / t[:, None])}


def reference(x, w0, w1):
    h = patch_conv_relu(f64(x), f64(w0))
    return patch_conv_relu(h, f64(w1))

@@ -1,0 +1,114 @@
+import math
+from contextlib import ExitStack
+
+import concourse.mybir as mybir
+from concourse.masks import make_identity
+
+BF16 = mybir.dt.bfloat16
+F32 = mybir.dt.float32
+U32 = mybir.dt.uint32
+U8 = mybir.dt.uint8
+FP8X4 = mybir.dt.float8_e4m3fn_x4
+RELU = mybir.ActivationFunctionType.Relu
+
+P = 128
+BATCH = 5
+CHANNELS = 256
+PAIR = CHANNELS // P
+TAPS = 2
+J = CHANNELS * TAPS
+D = 512
+Q = D // TAPS
+R = Q // TAPS
+SCALE = 1.0 / math.sqrt(CHANNELS)
+
+FLOPS = 2 * BATCH * (Q + R) * J * CHANNELS
+
+
+def quantise_weight(nc, pool, psum, identity, w):
+    raw = pool.tile([P, PAIR * J], BF16)
+    nc.sync.dma_start(out=raw[:], in_=w.rearrange("(m half) c k -> m (half c k)", half=PAIR))
+    words = raw[:].bitcast(F32).rearrange("m (half p u) -> m half u p", half=PAIR, u=PAIR)
+    flipped = psum.tile([P, PAIR, PAIR * P], F32)
+    for half in range(PAIR):
+        for u in range(PAIR):
+            nc.tensor.transpose(flipped[:, u, half * P : (half + 1) * P], words[:, half, u, :], identity[:])
+    grouped = pool.tile([P, PAIR * P * PAIR * TAPS], BF16, align_bytes=64)
+    nc.scalar.copy(
+        out=grouped[:].bitcast(F32).rearrange("p (col u) -> p col u", u=PAIR),
+        in_=flipped[:].rearrange("p u col -> p col u"),
+    )
+    codes = pool.tile([P, PAIR * P], U32, align_bytes=64)
+    scales = pool.tile([P, PAIR * P], U8, align_bytes=64)
+    nc.vector.quantize_mx(out=codes[:].bitcast(FP8X4), scales=scales[:], in_=grouped[:])
+    return codes, scales
+
+
+def conv_passes(nc, acc, w_codes, w_scales, codes, scales):
+    for half in range(PAIR):
+        m_cols = slice(half * P, (half + 1) * P)
+        nc.tensor.matmul_mx(
+            out=acc[:, half, :],
+            lhsT=w_codes[:, m_cols].bitcast(FP8X4),
+            lhsT_scale=w_scales[:, m_cols],
+            rhs=codes[:].bitcast(FP8X4),
+            rhs_scale=scales[:],
+            start=True,
+            stop=True,
+        )
+
+
+def tile_cnn_pa_s_kernel(tc, x, w0, w1, out):
+    nc = tc.nc
+    with ExitStack() as ctx:
+        consts = ctx.enter_context(tc.tile_pool(name="consts", bufs=1))
+        weights = ctx.enter_context(tc.tile_pool(name="weights", bufs=2))
+        batches = ctx.enter_context(tc.tile_pool(name="batches", bufs=BATCH))
+        psum_w = ctx.enter_context(tc.psum_pool(name="psum_w", bufs=2))
+        psum_h = ctx.enter_context(tc.psum_pool(name="psum_h", bufs=3))
+        psum_o = ctx.enter_context(tc.psum_pool(name="psum_o", bufs=3))
+
+        warm = consts.tile([P, 1], F32)
+        nc.vector.memset(warm[:], 0.0)
+        nc.scalar.activation(out=warm[:], in_=warm[:], func=RELU)
+
+        identity = consts.tile([P, P], F32)
+        make_identity(nc, identity[:])
+
+        w0_codes, w0_scales = quantise_weight(nc, weights, psum_w, identity, w0)
+        w1_codes, w1_scales = quantise_weight(nc, weights, psum_w, identity, w1)
+
+        for b in range(BATCH):
+            x_raw = batches.tile([P, PAIR * D], BF16)
+            nc.sync.dma_start(out=x_raw[:], in_=x[b].rearrange("(p u) d -> p (u d)", u=PAIR))
+            x_grouped = batches.tile([P, Q * PAIR * TAPS], BF16, align_bytes=64)
+            nc.vector.tensor_copy(
+                out=x_grouped[:].bitcast(F32).rearrange("p (q u) -> p q u", u=PAIR),
+                in_=x_raw[:].bitcast(F32).rearrange("p (u q) -> p q u", u=PAIR),
+            )
+            x_codes = batches.tile([P, Q], U32, align_bytes=64)
+            x_scales = batches.tile([P, Q], U8, align_bytes=64)
+            nc.vector.quantize_mx(out=x_codes[:].bitcast(FP8X4), scales=x_scales[:], in_=x_grouped[:])
+
+            h_acc = psum_h.tile([P, PAIR, Q], F32)
+            conv_passes(nc, h_acc, w0_codes, w0_scales, x_codes, x_scales)
+            h_grouped = batches.tile([P, R, PAIR, TAPS], BF16, align_bytes=64)
+            nc.scalar.activation(
+                out=h_grouped[:],
+                in_=h_acc[:].rearrange("p u (r k) -> p r u k", k=TAPS),
+                func=RELU,
+                scale=SCALE,
+            )
+            h_codes = batches.tile([P, R], U32, align_bytes=64)
+            h_scales = batches.tile([P, R], U8, align_bytes=64)
+            nc.vector.quantize_mx(
+                out=h_codes[:].bitcast(FP8X4),
+                scales=h_scales[:],
+                in_=h_grouped[:].rearrange("p r u k -> p (r u k)"),
+            )
+
+            o_acc = psum_o.tile([P, PAIR, R], F32)
+            conv_passes(nc, o_acc, w1_codes, w1_scales, h_codes, h_scales)
+            o_sb = batches.tile([P, PAIR, R], F32)
+            nc.scalar.activation(out=o_sb[:], in_=o_acc[:], func=RELU, scale=SCALE)
+            nc.sync.dma_start(out=out[b].rearrange("(m half) r -> m half r", half=PAIR), in_=o_sb[:])

@@ -16,6 +16,7 @@ BATCH = 5
 CHANNELS = 256
 PAIR = CHANNELS // P
 TAPS = 2
+WORD = PAIR * TAPS
 J = CHANNELS * TAPS
 D = 512
 Q = D // TAPS
@@ -25,26 +26,52 @@ SCALE = 1.0 / math.sqrt(CHANNELS)
 FLOPS = 2 * BATCH * (Q + R) * J * CHANNELS
 
 
-def quantise_weight(nc, pool, psum, identity, w):
-    raw = pool.tile([P, PAIR * J], BF16)
-    nc.sync.dma_start(out=raw[:], in_=w.rearrange("(m half) c k -> m (half c k)", half=PAIR))
-    words = raw[:].bitcast(F32).rearrange("m (half p u) -> m half u p", half=PAIR, u=PAIR)
+def load_weight(nc, pool, w):
+    w_raw = pool.tile([P, PAIR * J], BF16)
+    nc.sync.dma_start(out=w_raw[:], in_=w.rearrange("(m half) c k -> m (half c k)", half=PAIR))
+    return w_raw
+
+
+def load_x(nc, pool, x_b):
+    x_raw = pool.tile([P, PAIR * D], BF16)
+    nc.sync.dma_start(out=x_raw[:], in_=x_b.rearrange("(p u) d -> p (u d)", u=PAIR))
+    return x_raw
+
+
+def flip_weight(nc, pool, psum, identity, w_raw):
+    words = w_raw[:].bitcast(F32).rearrange("m (half p u) -> m half u p", half=PAIR, u=PAIR)
     flipped = psum.tile([P, PAIR, PAIR * P], F32)
     for half in range(PAIR):
         for u in range(PAIR):
             nc.tensor.transpose(flipped[:, u, half * P : (half + 1) * P], words[:, half, u, :], identity[:])
-    grouped = pool.tile([P, PAIR * P * PAIR * TAPS], BF16, align_bytes=64)
+    w_grouped = pool.tile([P, PAIR * P * WORD], BF16, align_bytes=64)
     nc.scalar.copy(
-        out=grouped[:].bitcast(F32).rearrange("p (col u) -> p col u", u=PAIR),
+        out=w_grouped[:].bitcast(F32).rearrange("p (col u) -> p col u", u=PAIR),
         in_=flipped[:].rearrange("p u col -> p col u"),
     )
-    codes = pool.tile([P, PAIR * P], U32, align_bytes=64)
-    scales = pool.tile([P, PAIR * P], U8, align_bytes=64)
+    return w_grouped
+
+
+def regroup_x(nc, pool, x_raw):
+    x_grouped = pool.tile([P, Q * WORD], BF16, align_bytes=64)
+    nc.vector.tensor_copy(
+        out=x_grouped[:].bitcast(F32).rearrange("p (q u) -> p q u", u=PAIR),
+        in_=x_raw[:].bitcast(F32).rearrange("p (u q) -> p q u", u=PAIR),
+    )
+    return x_grouped
+
+
+def quantise(nc, pool, grouped):
+    columns = grouped.shape[1] // WORD
+    codes = pool.tile([P, columns], U32, align_bytes=64)
+    scales = pool.tile([P, columns], U8, align_bytes=64)
     nc.vector.quantize_mx(out=codes[:].bitcast(FP8X4), scales=scales[:], in_=grouped[:])
     return codes, scales
 
 
-def conv_passes(nc, acc, w_codes, w_scales, codes, scales):
+def conv_passes(nc, acc, weight, operand):
+    w_codes, w_scales = weight
+    codes, scales = operand
     for half in range(PAIR):
         m_cols = slice(half * P, (half + 1) * P)
         nc.tensor.matmul_mx(
@@ -58,57 +85,66 @@ def conv_passes(nc, acc, w_codes, w_scales, codes, scales):
         )
 
 
+def layer1(nc, pool, psum, weight, x_mx):
+    h_acc = psum.tile([P, PAIR, Q], F32)
+    conv_passes(nc, h_acc, weight, x_mx)
+    h_grouped = pool.tile([P, R * WORD], BF16, align_bytes=64)
+    nc.scalar.activation(
+        out=h_grouped[:].rearrange("p (r u k) -> p r u k", u=PAIR, k=TAPS),
+        in_=h_acc[:].rearrange("p u (r k) -> p r u k", k=TAPS),
+        func=RELU,
+        scale=SCALE,
+    )
+    return h_grouped
+
+
+def layer2(nc, pool, psum, weight, h_mx, out_b):
+    o_acc = psum.tile([P, PAIR, R], F32)
+    conv_passes(nc, o_acc, weight, h_mx)
+    o_sb = pool.tile([P, PAIR, R], F32)
+    nc.scalar.activation(out=o_sb[:], in_=o_acc[:], func=RELU, scale=SCALE)
+    nc.sync.dma_start(out=out_b.rearrange("(m half) r -> m half r", half=PAIR), in_=o_sb[:])
+
+
 def tile_cnn_pa_s_kernel(tc, x, w0, w1, out):
     nc = tc.nc
     with ExitStack() as ctx:
         consts = ctx.enter_context(tc.tile_pool(name="consts", bufs=1))
         weights = ctx.enter_context(tc.tile_pool(name="weights", bufs=2))
-        batches = ctx.enter_context(tc.tile_pool(name="batches", bufs=BATCH))
+        xs = ctx.enter_context(tc.tile_pool(name="xs", bufs=BATCH))
+        hs = ctx.enter_context(tc.tile_pool(name="hs", bufs=BATCH))
+        outs = ctx.enter_context(tc.tile_pool(name="outs", bufs=BATCH))
         psum_w = ctx.enter_context(tc.psum_pool(name="psum_w", bufs=2))
         psum_h = ctx.enter_context(tc.psum_pool(name="psum_h", bufs=3))
         psum_o = ctx.enter_context(tc.psum_pool(name="psum_o", bufs=3))
+        ctx.enter_context(tc.manual_schedule())
+
+        w0_raw = load_weight(nc, weights, w0)
+        x_raw = [load_x(nc, xs, x[0])]
+        w1_raw = load_weight(nc, weights, w1)
+        for b in range(1, BATCH):
+            x_raw.append(load_x(nc, xs, x[b]))
 
         warm = consts.tile([P, 1], F32)
         nc.vector.memset(warm[:], 0.0)
         nc.scalar.activation(out=warm[:], in_=warm[:], func=RELU)
-
         identity = consts.tile([P, P], F32)
         make_identity(nc, identity[:])
 
-        w0_codes, w0_scales = quantise_weight(nc, weights, psum_w, identity, w0)
-        w1_codes, w1_scales = quantise_weight(nc, weights, psum_w, identity, w1)
+        w0_grouped = flip_weight(nc, weights, psum_w, identity, w0_raw)
+        x_mx = [quantise(nc, xs, regroup_x(nc, xs, x_raw[0]))]
+        w0_mx = quantise(nc, weights, w0_grouped)
+        w1_grouped = flip_weight(nc, weights, psum_w, identity, w1_raw)
+        x_mx.append(quantise(nc, xs, regroup_x(nc, xs, x_raw[1])))
+        w1_mx = quantise(nc, weights, w1_grouped)
 
+        h_grouped = [layer1(nc, hs, psum_h, w0_mx, x_mx[0])]
         for b in range(BATCH):
-            x_raw = batches.tile([P, PAIR * D], BF16)
-            nc.sync.dma_start(out=x_raw[:], in_=x[b].rearrange("(p u) d -> p (u d)", u=PAIR))
-            x_grouped = batches.tile([P, Q * PAIR * TAPS], BF16, align_bytes=64)
-            nc.vector.tensor_copy(
-                out=x_grouped[:].bitcast(F32).rearrange("p (q u) -> p q u", u=PAIR),
-                in_=x_raw[:].bitcast(F32).rearrange("p (u q) -> p q u", u=PAIR),
-            )
-            x_codes = batches.tile([P, Q], U32, align_bytes=64)
-            x_scales = batches.tile([P, Q], U8, align_bytes=64)
-            nc.vector.quantize_mx(out=x_codes[:].bitcast(FP8X4), scales=x_scales[:], in_=x_grouped[:])
-
-            h_acc = psum_h.tile([P, PAIR, Q], F32)
-            conv_passes(nc, h_acc, w0_codes, w0_scales, x_codes, x_scales)
-            h_grouped = batches.tile([P, R, PAIR, TAPS], BF16, align_bytes=64)
-            nc.scalar.activation(
-                out=h_grouped[:],
-                in_=h_acc[:].rearrange("p u (r k) -> p r u k", k=TAPS),
-                func=RELU,
-                scale=SCALE,
-            )
-            h_codes = batches.tile([P, R], U32, align_bytes=64)
-            h_scales = batches.tile([P, R], U8, align_bytes=64)
-            nc.vector.quantize_mx(
-                out=h_codes[:].bitcast(FP8X4),
-                scales=h_scales[:],
-                in_=h_grouped[:].rearrange("p r u k -> p (r u k)"),
-            )
-
-            o_acc = psum_o.tile([P, PAIR, R], F32)
-            conv_passes(nc, o_acc, w1_codes, w1_scales, h_codes, h_scales)
-            o_sb = batches.tile([P, PAIR, R], F32)
-            nc.scalar.activation(out=o_sb[:], in_=o_acc[:], func=RELU, scale=SCALE)
-            nc.sync.dma_start(out=out[b].rearrange("(m half) r -> m half r", half=PAIR), in_=o_sb[:])
+            if b + 1 < BATCH:
+                h_grouped.append(layer1(nc, hs, psum_h, w0_mx, x_mx[b + 1]))
+            if b + 2 < BATCH:
+                x_grouped = regroup_x(nc, xs, x_raw[b + 2])
+            h_mx = quantise(nc, hs, h_grouped[b])
+            if b + 2 < BATCH:
+                x_mx.append(quantise(nc, xs, x_grouped))
+            layer2(nc, outs, psum_o, w1_mx, h_mx, out[b])

@@ -106,6 +106,9 @@ def layer2(nc, pool, psum, weight, h_mx, out_b):
     nc.sync.dma_start(out=out_b.rearrange("(m half) r -> m half r", half=PAIR), in_=o_sb[:])
 
 
+AHEAD = 2
+
+
 def tile_cnn_pa_s_kernel(tc, x, w0, w1, out):
     nc = tc.nc
     with ExitStack() as ctx:
@@ -132,19 +135,20 @@ def tile_cnn_pa_s_kernel(tc, x, w0, w1, out):
         make_identity(nc, identity[:])
 
         w0_grouped = flip_weight(nc, weights, psum_w, identity, w0_raw)
+        w1_grouped = flip_weight(nc, weights, psum_w, identity, w1_raw)
         x_mx = [quantise(nc, xs, regroup_x(nc, xs, x_raw[0]))]
         w0_mx = quantise(nc, weights, w0_grouped)
-        w1_grouped = flip_weight(nc, weights, psum_w, identity, w1_raw)
-        x_mx.append(quantise(nc, xs, regroup_x(nc, xs, x_raw[1])))
+        for b in range(1, AHEAD + 1):
+            x_mx.append(quantise(nc, xs, regroup_x(nc, xs, x_raw[b])))
         w1_mx = quantise(nc, weights, w1_grouped)
 
-        h_grouped = [layer1(nc, hs, psum_h, w0_mx, x_mx[0])]
+        h_grouped = [layer1(nc, hs, psum_h, w0_mx, x_mx[b]) for b in range(AHEAD)]
         for b in range(BATCH):
-            if b + 1 < BATCH:
-                h_grouped.append(layer1(nc, hs, psum_h, w0_mx, x_mx[b + 1]))
-            if b + 2 < BATCH:
-                x_grouped = regroup_x(nc, xs, x_raw[b + 2])
+            if b + AHEAD < BATCH:
+                h_grouped.append(layer1(nc, hs, psum_h, w0_mx, x_mx[b + AHEAD]))
+            if b + AHEAD + 1 < BATCH:
+                x_grouped = regroup_x(nc, xs, x_raw[b + AHEAD + 1])
             h_mx = quantise(nc, hs, h_grouped[b])
-            if b + 2 < BATCH:
+            if b + AHEAD + 1 < BATCH:
                 x_mx.append(quantise(nc, xs, x_grouped))
             layer2(nc, outs, psum_o, w1_mx, h_mx, out[b])

@@ -12,6 +12,7 @@ FP8X4 = mybir.dt.float8_e4m3fn_x4
 RELU = mybir.ActivationFunctionType.Relu
 
 P = 128
+PSUM_BANKS = 8
 BATCH = 5
 CHANNELS = 256
 PAIR = CHANNELS // P
@@ -40,7 +41,7 @@ def load_x(nc, pool, x_b):
 
 def flip_weight(nc, pool, psum, identity, w_raw):
     words = w_raw[:].bitcast(F32).rearrange("m (half p u) -> m half u p", half=PAIR, u=PAIR)
-    flipped = psum.tile([P, PAIR, PAIR * P], F32)
+    flipped = psum.tile([P, PAIR, PAIR * P], F32, tag="bank")
     for half in range(PAIR):
         for u in range(PAIR):
             nc.tensor.transpose(flipped[:, u, half * P : (half + 1) * P], words[:, half, u, :], identity[:])
@@ -86,7 +87,7 @@ def conv_passes(nc, acc, weight, operand):
 
 
 def layer1(nc, pool, psum, weight, x_mx):
-    h_acc = psum.tile([P, PAIR, Q], F32)
+    h_acc = psum.tile([P, PAIR, Q], F32, tag="bank")
     conv_passes(nc, h_acc, weight, x_mx)
     h_grouped = pool.tile([P, R * WORD], BF16, align_bytes=64)
     nc.scalar.activation(
@@ -99,14 +100,11 @@ def layer1(nc, pool, psum, weight, x_mx):
 
 
 def layer2(nc, pool, psum, weight, h_mx, out_b):
-    o_acc = psum.tile([P, PAIR, R], F32)
+    o_acc = psum.tile([P, PAIR, R], F32, tag="bank")
     conv_passes(nc, o_acc, weight, h_mx)
     o_sb = pool.tile([P, PAIR, R], F32)
     nc.scalar.activation(out=o_sb[:], in_=o_acc[:], func=RELU, scale=SCALE)
     nc.sync.dma_start(out=out_b.rearrange("(m half) r -> m half r", half=PAIR), in_=o_sb[:])
-
-
-AHEAD = 2
 
 
 def tile_cnn_pa_s_kernel(tc, x, w0, w1, out):
@@ -117,15 +115,13 @@ def tile_cnn_pa_s_kernel(tc, x, w0, w1, out):
         xs = ctx.enter_context(tc.tile_pool(name="xs", bufs=BATCH))
         hs = ctx.enter_context(tc.tile_pool(name="hs", bufs=BATCH))
         outs = ctx.enter_context(tc.tile_pool(name="outs", bufs=BATCH))
-        psum_w = ctx.enter_context(tc.psum_pool(name="psum_w", bufs=2))
-        psum_h = ctx.enter_context(tc.psum_pool(name="psum_h", bufs=3))
-        psum_o = ctx.enter_context(tc.psum_pool(name="psum_o", bufs=3))
+        psum = ctx.enter_context(tc.psum_pool(name="psum", bufs=PSUM_BANKS))
         ctx.enter_context(tc.manual_schedule())
 
         w0_raw = load_weight(nc, weights, w0)
-        x_raw = [load_x(nc, xs, x[0])]
+        x_raw = [load_x(nc, xs, x[b]) for b in range(2)]
         w1_raw = load_weight(nc, weights, w1)
-        for b in range(1, BATCH):
+        for b in range(2, BATCH):
             x_raw.append(load_x(nc, xs, x[b]))
 
         warm = consts.tile([P, 1], F32)
@@ -134,21 +130,20 @@ def tile_cnn_pa_s_kernel(tc, x, w0, w1, out):
         identity = consts.tile([P, P], F32)
         make_identity(nc, identity[:])
 
-        w0_grouped = flip_weight(nc, weights, psum_w, identity, w0_raw)
-        w1_grouped = flip_weight(nc, weights, psum_w, identity, w1_raw)
-        x_mx = [quantise(nc, xs, regroup_x(nc, xs, x_raw[0]))]
-        w0_mx = quantise(nc, weights, w0_grouped)
-        for b in range(1, AHEAD + 1):
-            x_mx.append(quantise(nc, xs, regroup_x(nc, xs, x_raw[b])))
-        w1_mx = quantise(nc, weights, w1_grouped)
+        w0_grouped = flip_weight(nc, weights, psum, identity, w0_raw)
+        w1_grouped = flip_weight(nc, weights, psum, identity, w1_raw)
 
-        h_grouped = [layer1(nc, hs, psum_h, w0_mx, x_mx[b]) for b in range(AHEAD)]
+        x_grouped = [regroup_x(nc, xs, x_raw[0])]
+        h_grouped = []
         for b in range(BATCH):
-            if b + AHEAD < BATCH:
-                h_grouped.append(layer1(nc, hs, psum_h, w0_mx, x_mx[b + AHEAD]))
-            if b + AHEAD + 1 < BATCH:
-                x_grouped = regroup_x(nc, xs, x_raw[b + AHEAD + 1])
+            if b + 1 < BATCH:
+                x_grouped.append(regroup_x(nc, xs, x_raw[b + 1]))
+            if b == 0:
+                w0_mx = quantise(nc, weights, w0_grouped)
+            x_mx = quantise(nc, xs, x_grouped[b])
+            h_grouped.append(layer1(nc, hs, psum, w0_mx, x_mx))
+
+        w1_mx = quantise(nc, weights, w1_grouped)
+        for b in range(BATCH):
             h_mx = quantise(nc, hs, h_grouped[b])
-            if b + AHEAD + 1 < BATCH:
-                x_mx.append(quantise(nc, xs, x_grouped))
-            layer2(nc, outs, psum_o, w1_mx, h_mx, out[b])
+            layer2(nc, outs, psum, w1_mx, h_mx, out[b])

@@ -13,6 +13,8 @@ RELU = mybir.ActivationFunctionType.Relu
 
 P = 128
 PSUM_BANKS = 8
+MX_ALIGN = 64
+LAYERS = 2
 BATCH = 5
 CHANNELS = 256
 PAIR = CHANNELS // P
@@ -23,6 +25,7 @@ D = 512
 Q = D // TAPS
 R = Q // TAPS
 SCALE = 1.0 / math.sqrt(CHANNELS)
+COPY_AHEAD = 1
 
 FLOPS = 2 * BATCH * (Q + R) * J * CHANNELS
 
@@ -45,7 +48,7 @@ def flip_weight(nc, pool, psum, identity, w_raw):
     for half in range(PAIR):
         for u in range(PAIR):
             nc.tensor.transpose(flipped[:, u, half * P : (half + 1) * P], words[:, half, u, :], identity[:])
-    w_grouped = pool.tile([P, PAIR * P * WORD], BF16, align_bytes=64)
+    w_grouped = pool.tile([P, PAIR * P * WORD], BF16, align_bytes=MX_ALIGN)
     nc.scalar.copy(
         out=w_grouped[:].bitcast(F32).rearrange("p (col u) -> p col u", u=PAIR),
         in_=flipped[:].rearrange("p u col -> p col u"),
@@ -54,7 +57,7 @@ def flip_weight(nc, pool, psum, identity, w_raw):
 
 
 def regroup_x(nc, pool, x_raw):
-    x_grouped = pool.tile([P, Q * WORD], BF16, align_bytes=64)
+    x_grouped = pool.tile([P, Q * WORD], BF16, align_bytes=MX_ALIGN)
     nc.vector.tensor_copy(
         out=x_grouped[:].bitcast(F32).rearrange("p (q u) -> p q u", u=PAIR),
         in_=x_raw[:].bitcast(F32).rearrange("p (u q) -> p q u", u=PAIR),
@@ -64,15 +67,15 @@ def regroup_x(nc, pool, x_raw):
 
 def quantise(nc, pool, grouped):
     columns = grouped.shape[1] // WORD
-    codes = pool.tile([P, columns], U32, align_bytes=64)
-    scales = pool.tile([P, columns], U8, align_bytes=64)
+    codes = pool.tile([P, columns], U32, align_bytes=MX_ALIGN)
+    scales = pool.tile([P, columns], U8, align_bytes=MX_ALIGN)
     nc.vector.quantize_mx(out=codes[:].bitcast(FP8X4), scales=scales[:], in_=grouped[:])
     return codes, scales
 
 
-def conv_passes(nc, acc, weight, operand):
-    w_codes, w_scales = weight
-    codes, scales = operand
+def conv_passes(nc, acc, w_mx, operand_mx):
+    w_codes, w_scales = w_mx
+    codes, scales = operand_mx
     for half in range(PAIR):
         m_cols = slice(half * P, (half + 1) * P)
         nc.tensor.matmul_mx(
@@ -86,10 +89,10 @@ def conv_passes(nc, acc, weight, operand):
         )
 
 
-def layer1(nc, pool, psum, weight, x_mx):
+def layer1(nc, pool, psum, w_mx, x_mx):
     h_acc = psum.tile([P, PAIR, Q], F32, tag="bank")
-    conv_passes(nc, h_acc, weight, x_mx)
-    h_grouped = pool.tile([P, R * WORD], BF16, align_bytes=64)
+    conv_passes(nc, h_acc, w_mx, x_mx)
+    h_grouped = pool.tile([P, R * WORD], BF16, align_bytes=MX_ALIGN)
     nc.scalar.activation(
         out=h_grouped[:].rearrange("p (r u k) -> p r u k", u=PAIR, k=TAPS),
         in_=h_acc[:].rearrange("p u (r k) -> p r u k", k=TAPS),
@@ -99,9 +102,9 @@ def layer1(nc, pool, psum, weight, x_mx):
     return h_grouped
 
 
-def layer2(nc, pool, psum, weight, h_mx, out_b):
+def layer2(nc, pool, psum, w_mx, h_mx, out_b):
     o_acc = psum.tile([P, PAIR, R], F32, tag="bank")
-    conv_passes(nc, o_acc, weight, h_mx)
+    conv_passes(nc, o_acc, w_mx, h_mx)
     o_sb = pool.tile([P, PAIR, R], F32)
     nc.scalar.activation(out=o_sb[:], in_=o_acc[:], func=RELU, scale=SCALE)
     nc.sync.dma_start(out=out_b.rearrange("(m half) r -> m half r", half=PAIR), in_=o_sb[:])
@@ -111,7 +114,7 @@ def tile_cnn_pa_s_kernel(tc, x, w0, w1, out):
     nc = tc.nc
     with ExitStack() as ctx:
         consts = ctx.enter_context(tc.tile_pool(name="consts", bufs=1))
-        weights = ctx.enter_context(tc.tile_pool(name="weights", bufs=2))
+        weights = ctx.enter_context(tc.tile_pool(name="weights", bufs=LAYERS))
         xs = ctx.enter_context(tc.tile_pool(name="xs", bufs=BATCH))
         hs = ctx.enter_context(tc.tile_pool(name="hs", bufs=BATCH))
         outs = ctx.enter_context(tc.tile_pool(name="outs", bufs=BATCH))
@@ -119,10 +122,9 @@ def tile_cnn_pa_s_kernel(tc, x, w0, w1, out):
         ctx.enter_context(tc.manual_schedule())
 
         w0_raw = load_weight(nc, weights, w0)
-        x_raw = [load_x(nc, xs, x[b]) for b in range(2)]
+        x_raw = [load_x(nc, xs, x[b]) for b in range(COPY_AHEAD + 1)]
         w1_raw = load_weight(nc, weights, w1)
-        for b in range(2, BATCH):
-            x_raw.append(load_x(nc, xs, x[b]))
+        x_raw.extend([load_x(nc, xs, x[b]) for b in range(COPY_AHEAD + 1, BATCH)])
 
         warm = consts.tile([P, 1], F32)
         nc.vector.memset(warm[:], 0.0)
@@ -133,15 +135,14 @@ def tile_cnn_pa_s_kernel(tc, x, w0, w1, out):
         w0_grouped = flip_weight(nc, weights, psum, identity, w0_raw)
         w1_grouped = flip_weight(nc, weights, psum, identity, w1_raw)
 
-        x_grouped = [regroup_x(nc, xs, x_raw[0])]
+        x_grouped = [regroup_x(nc, xs, x_raw[b]) for b in range(COPY_AHEAD + 1)]
+        w0_mx = quantise(nc, weights, w0_grouped)
         h_grouped = []
         for b in range(BATCH):
-            if b + 1 < BATCH:
-                x_grouped.append(regroup_x(nc, xs, x_raw[b + 1]))
-            if b == 0:
-                w0_mx = quantise(nc, weights, w0_grouped)
             x_mx = quantise(nc, xs, x_grouped[b])
             h_grouped.append(layer1(nc, hs, psum, w0_mx, x_mx))
+            if b + COPY_AHEAD + 1 < BATCH:
+                x_grouped.append(regroup_x(nc, xs, x_raw[b + COPY_AHEAD + 1]))
 
         w1_mx = quantise(nc, weights, w1_grouped)
         for b in range(BATCH):

@@ -136,10 +136,12 @@ def tile_cnn_pa_s_kernel(tc, x, w0, w1, out):
         w1_grouped = flip_weight(nc, weights, psum, identity, w1_raw)
 
         x_grouped = [regroup_x(nc, xs, x_raw[b]) for b in range(COPY_AHEAD + 1)]
+        x_mx = quantise(nc, xs, x_grouped[0])
         w0_mx = quantise(nc, weights, w0_grouped)
         h_grouped = []
         for b in range(BATCH):
-            x_mx = quantise(nc, xs, x_grouped[b])
+            if b > 0:
+                x_mx = quantise(nc, xs, x_grouped[b])
             h_grouped.append(layer1(nc, hs, psum, w0_mx, x_mx))
             if b + COPY_AHEAD + 1 < BATCH:
                 x_grouped.append(regroup_x(nc, xs, x_raw[b + COPY_AHEAD + 1]))

@@ -25,14 +25,19 @@ D = 512
 Q = D // TAPS
 R = Q // TAPS
 SCALE = 1.0 / math.sqrt(CHANNELS)
+ALU = mybir.AluOpType
 COPY_AHEAD = 1
 
 FLOPS = 2 * BATCH * (Q + R) * J * CHANNELS
 
 
 def load_weight(nc, pool, w):
-    w_raw = pool.tile([P, PAIR * J], BF16)
-    nc.sync.dma_start(out=w_raw[:], in_=w.rearrange("(m half) c k -> m (half c k)", half=PAIR))
+    halves = w.rearrange("(m half) c k -> half m (c k)", half=PAIR)
+    w_raw = []
+    for half in range(PAIR):
+        raw = pool.tile([P, J], BF16, tag="w_raw")
+        nc.sync.dma_start(out=raw[:], in_=halves[half])
+        w_raw.append(raw)
     return w_raw
 
 
@@ -42,13 +47,12 @@ def load_x(nc, pool, x_b):
     return x_raw
 
 
-def flip_weight(nc, pool, psum, identity, w_raw):
-    words = w_raw[:].bitcast(F32).rearrange("m (half p u) -> m half u p", half=PAIR, u=PAIR)
-    flipped = psum.tile([P, PAIR, PAIR * P], F32, tag="bank")
-    for half in range(PAIR):
-        for u in range(PAIR):
-            nc.tensor.transpose(flipped[:, u, half * P : (half + 1) * P], words[:, half, u, :], identity[:])
-    w_grouped = pool.tile([P, PAIR * P * WORD], BF16, align_bytes=MX_ALIGN)
+def flip_weight(nc, pool, psum, identity, raw):
+    words = raw[:].bitcast(F32).rearrange("m (p u) -> m u p", u=PAIR)
+    flipped = psum.tile([P, PAIR, P], F32, tag="bank")
+    for u in range(PAIR):
+        nc.tensor.transpose(flipped[:, u, :], words[:, u, :], identity[:])
+    w_grouped = pool.tile([P, P * WORD], BF16, align_bytes=MX_ALIGN)
     nc.scalar.copy(
         out=w_grouped[:].bitcast(F32).rearrange("p (col u) -> p col u", u=PAIR),
         in_=flipped[:].rearrange("p u col -> p col u"),
@@ -74,14 +78,13 @@ def quantise(nc, pool, grouped):
 
 
 def conv_passes(nc, acc, w_mx, operand_mx):
-    w_codes, w_scales = w_mx
     codes, scales = operand_mx
     for half in range(PAIR):
-        m_cols = slice(half * P, (half + 1) * P)
+        w_codes, w_scales = w_mx[half]
         nc.tensor.matmul_mx(
             out=acc[:, half, :],
-            lhsT=w_codes[:, m_cols].bitcast(FP8X4),
-            lhsT_scale=w_scales[:, m_cols],
+            lhsT=w_codes[:].bitcast(FP8X4),
+            lhsT_scale=w_scales[:],
             rhs=codes[:].bitcast(FP8X4),
             rhs_scale=scales[:],
             start=True,
@@ -102,11 +105,18 @@ def layer1(nc, pool, psum, w_mx, x_mx):
     return h_grouped
 
 
-def layer2(nc, pool, psum, w_mx, h_mx, out_b):
+def layer2(nc, psum, w_mx, h_mx):
     o_acc = psum.tile([P, PAIR, R], F32, tag="bank")
     conv_passes(nc, o_acc, w_mx, h_mx)
+    return o_acc
+
+
+def finish(nc, pool, o_acc, out_b, on_vector):
     o_sb = pool.tile([P, PAIR, R], F32)
-    nc.scalar.activation(out=o_sb[:], in_=o_acc[:], func=RELU, scale=SCALE)
+    if on_vector:
+        nc.vector.tensor_scalar(out=o_sb[:], in0=o_acc[:], scalar1=SCALE, scalar2=0.0, op0=ALU.mult, op1=ALU.max)
+    else:
+        nc.scalar.activation(out=o_sb[:], in_=o_acc[:], func=RELU, scale=SCALE)
     nc.sync.dma_start(out=out_b.rearrange("(m half) r -> m half r", half=PAIR), in_=o_sb[:])
 
 
@@ -114,7 +124,7 @@ def tile_cnn_pa_s_kernel(tc, x, w0, w1, out):
     nc = tc.nc
     with ExitStack() as ctx:
         consts = ctx.enter_context(tc.tile_pool(name="consts", bufs=1))
-        weights = ctx.enter_context(tc.tile_pool(name="weights", bufs=LAYERS))
+        weights = ctx.enter_context(tc.tile_pool(name="weights", bufs=LAYERS * PAIR))
         xs = ctx.enter_context(tc.tile_pool(name="xs", bufs=BATCH))
         hs = ctx.enter_context(tc.tile_pool(name="hs", bufs=BATCH))
         outs = ctx.enter_context(tc.tile_pool(name="outs", bufs=BATCH))
@@ -122,9 +132,9 @@ def tile_cnn_pa_s_kernel(tc, x, w0, w1, out):
         ctx.enter_context(tc.manual_schedule())
 
         w0_raw = load_weight(nc, weights, w0)
-        x_raw = [load_x(nc, xs, x[b]) for b in range(COPY_AHEAD + 1)]
+        x_raw = [load_x(nc, xs, x[0])]
         w1_raw = load_weight(nc, weights, w1)
-        x_raw.extend([load_x(nc, xs, x[b]) for b in range(COPY_AHEAD + 1, BATCH)])
+        x_raw.extend([load_x(nc, xs, x[b]) for b in range(1, BATCH)])
 
         warm = consts.tile([P, 1], F32)
         nc.vector.memset(warm[:], 0.0)
@@ -132,21 +142,28 @@ def tile_cnn_pa_s_kernel(tc, x, w0, w1, out):
         identity = consts.tile([P, P], F32)
         make_identity(nc, identity[:])
 
-        w0_grouped = flip_weight(nc, weights, psum, identity, w0_raw)
-        w1_grouped = flip_weight(nc, weights, psum, identity, w1_raw)
+        w0_grouped = [flip_weight(nc, weights, psum, identity, raw) for raw in w0_raw]
+        w1_grouped = [flip_weight(nc, weights, psum, identity, raw) for raw in w1_raw]
 
-        x_grouped = [regroup_x(nc, xs, x_raw[b]) for b in range(COPY_AHEAD + 1)]
+        x_grouped = [regroup_x(nc, xs, x_raw[0])]
+        w0_mx = [quantise(nc, weights, w0_grouped[0])]
         x_mx = quantise(nc, xs, x_grouped[0])
-        w0_mx = quantise(nc, weights, w0_grouped)
-        h_grouped = []
-        for b in range(BATCH):
-            if b > 0:
-                x_mx = quantise(nc, xs, x_grouped[b])
+        w0_mx.append(quantise(nc, weights, w0_grouped[1]))
+        x_grouped.append(regroup_x(nc, xs, x_raw[1]))
+        h_grouped = [layer1(nc, hs, psum, w0_mx, x_mx)]
+        for b in range(1, BATCH):
+            if b + 1 < BATCH:
+                x_grouped.append(regroup_x(nc, xs, x_raw[b + 1]))
+            else:
+                w1_mx = [quantise(nc, weights, grouped) for grouped in w1_grouped]
+            x_mx = quantise(nc, xs, x_grouped[b])
             h_grouped.append(layer1(nc, hs, psum, w0_mx, x_mx))
-            if b + COPY_AHEAD + 1 < BATCH:
-                x_grouped.append(regroup_x(nc, xs, x_raw[b + COPY_AHEAD + 1]))
 
-        w1_mx = quantise(nc, weights, w1_grouped)
+        o_acc = []
         for b in range(BATCH):
             h_mx = quantise(nc, hs, h_grouped[b])
-            layer2(nc, outs, psum, w1_mx, h_mx, out[b])
+            o_acc.append(layer2(nc, psum, w1_mx, h_mx))
+            if b == 2 or b == 3:
+                finish(nc, outs, o_acc[b - 2], out[b - 2], True)
+        for b in range(2, BATCH):
+            finish(nc, outs, o_acc[b], out[b], b == 3)

@@ -26,6 +26,7 @@ Q = D // TAPS
 R = Q // TAPS
 SCALE = 1.0 / math.sqrt(CHANNELS)
 ALU = mybir.AluOpType
+WARM_UPS = 4
 COPY_AHEAD = 1
 
 FLOPS = 2 * BATCH * (Q + R) * J * CHANNELS
@@ -141,6 +142,12 @@ def tile_cnn_pa_s_kernel(tc, x, w0, w1, out):
         nc.scalar.activation(out=warm[:], in_=warm[:], func=RELU)
         identity = consts.tile([P, P], F32)
         make_identity(nc, identity[:])
+
+        zeros = consts.tile([P, P], F32)
+        nc.vector.memset(zeros[:], 0.0)
+        scratch = psum.tile([P, P], F32, tag="bank")
+        for i in range(WARM_UPS):
+            nc.tensor.matmul(scratch[:], lhsT=zeros[:], rhs=zeros[:], start=True, stop=True)
 
         w0_grouped = [flip_weight(nc, weights, psum, identity, raw) for raw in w0_raw]
         w1_grouped = [flip_weight(nc, weights, psum, identity, raw) for raw in w1_raw]

@@ -26,7 +26,7 @@ Q = D // TAPS
 R = Q // TAPS
 SCALE = 1.0 / math.sqrt(CHANNELS)
 ALU = mybir.AluOpType
-WARM_UPS = 4
+WARM_UPS = 2
 COPY_AHEAD = 1
 
 FLOPS = 2 * BATCH * (Q + R) * J * CHANNELS
@@ -161,11 +161,10 @@ def tile_cnn_pa_s_kernel(tc, x, w0, w1, out):
         for b in range(1, BATCH):
             if b + 1 < BATCH:
                 x_grouped.append(regroup_x(nc, xs, x_raw[b + 1]))
-            else:
-                w1_mx = [quantise(nc, weights, grouped) for grouped in w1_grouped]
             x_mx = quantise(nc, xs, x_grouped[b])
             h_grouped.append(layer1(nc, hs, psum, w0_mx, x_mx))
 
+        w1_mx = [quantise(nc, weights, grouped) for grouped in w1_grouped]
         o_acc = []
         for b in range(BATCH):
             h_mx = quantise(nc, hs, h_grouped[b])

@@ -26,7 +26,7 @@ Q = D // TAPS
 R = Q // TAPS
 SCALE = 1.0 / math.sqrt(CHANNELS)
 ALU = mybir.AluOpType
-WARM_UPS = 2
+WARM_UPS = 3
 COPY_AHEAD = 1
 
 FLOPS = 2 * BATCH * (Q + R) * J * CHANNELS
@@ -93,6 +93,11 @@ def conv_passes(nc, acc, w_mx, operand_mx):
         )
 
 
+def warm_up(nc, scratch, zeros, count):
+    for i in range(count):
+        nc.tensor.matmul(scratch[:], lhsT=zeros[:], rhs=zeros[:], start=True, stop=True)
+
+
 def layer1(nc, pool, psum, w_mx, x_mx):
     h_acc = psum.tile([P, PAIR, Q], F32, tag="bank")
     conv_passes(nc, h_acc, w_mx, x_mx)
@@ -137,19 +142,18 @@ def tile_cnn_pa_s_kernel(tc, x, w0, w1, out):
         w1_raw = load_weight(nc, weights, w1)
         x_raw.extend([load_x(nc, xs, x[b]) for b in range(1, BATCH)])
 
+        zeros = consts.tile([P, P], F32)
+        nc.vector.memset(zeros[:], 0.0)
         warm = consts.tile([P, 1], F32)
         nc.vector.memset(warm[:], 0.0)
         nc.scalar.activation(out=warm[:], in_=warm[:], func=RELU)
         identity = consts.tile([P, P], F32)
         make_identity(nc, identity[:])
 
-        zeros = consts.tile([P, P], F32)
-        nc.vector.memset(zeros[:], 0.0)
         scratch = psum.tile([P, P], F32, tag="bank")
-        for i in range(WARM_UPS):
-            nc.tensor.matmul(scratch[:], lhsT=zeros[:], rhs=zeros[:], start=True, stop=True)
-
+        warm_up(nc, scratch, zeros, WARM_UPS)
         w0_grouped = [flip_weight(nc, weights, psum, identity, raw) for raw in w0_raw]
+        warm_up(nc, scratch, zeros, 1)
         w1_grouped = [flip_weight(nc, weights, psum, identity, raw) for raw in w1_raw]
 
         x_grouped = [regroup_x(nc, xs, x_raw[0])]

@@ -123,7 +123,8 @@ def finish(nc, pool, o_acc, out_b, on_vector):
         nc.vector.tensor_scalar(out=o_sb[:], in0=o_acc[:], scalar1=SCALE, scalar2=0.0, op0=ALU.mult, op1=ALU.max)
     else:
         nc.scalar.activation(out=o_sb[:], in_=o_acc[:], func=RELU, scale=SCALE)
-    nc.sync.dma_start(out=out_b.rearrange("(m half) r -> m half r", half=PAIR), in_=o_sb[:])
+    queue = nc.sync if on_vector else nc.scalar
+    queue.dma_start(out=out_b.rearrange("(m half) r -> m half r", half=PAIR), in_=o_sb[:])
 
 
 def tile_cnn_pa_s_kernel(tc, x, w0, w1, out):
@@ -153,7 +154,7 @@ def tile_cnn_pa_s_kernel(tc, x, w0, w1, out):
         scratch = psum.tile([P, P], F32, tag="bank")
         warm_up(nc, scratch, zeros, WARM_UPS)
         w0_grouped = [flip_weight(nc, weights, psum, identity, raw) for raw in w0_raw]
-        warm_up(nc, scratch, zeros, 1)
+        warm_up(nc, scratch, zeros, 2)
         w1_grouped = [flip_weight(nc, weights, psum, identity, raw) for raw in w1_raw]
 
         x_grouped = [regroup_x(nc, xs, x_raw[0])]

import math
from contextlib import ExitStack

import concourse.mybir as mybir
from concourse.masks import make_identity

BF16 = mybir.dt.bfloat16
F32 = mybir.dt.float32
U32 = mybir.dt.uint32
U8 = mybir.dt.uint8
FP8X4 = mybir.dt.float8_e4m3fn_x4
RELU = mybir.ActivationFunctionType.Relu

P = 128
PSUM_BANKS = 8
MX_ALIGN = 64
LAYERS = 2
BATCH = 5
CHANNELS = 256
PAIR = CHANNELS // P
TAPS = 2
WORD = PAIR * TAPS
J = CHANNELS * TAPS
D = 512
Q = D // TAPS
R = Q // TAPS
SCALE = 1.0 / math.sqrt(CHANNELS)
ALU = mybir.AluOpType
WARM_UPS = 3
COPY_AHEAD = 1

FLOPS = 2 * BATCH * (Q + R) * J * CHANNELS


def load_weight(nc, pool, w):
    halves = w.rearrange("(m half) c k -> half m (c k)", half=PAIR)
    w_raw = []
    for half in range(PAIR):
        raw = pool.tile([P, J], BF16, tag="w_raw")
        nc.sync.dma_start(out=raw[:], in_=halves[half])
        w_raw.append(raw)
    return w_raw


def load_x(nc, pool, x_b):
    x_raw = pool.tile([P, PAIR * D], BF16)
    nc.sync.dma_start(out=x_raw[:], in_=x_b.rearrange("(p u) d -> p (u d)", u=PAIR))
    return x_raw


def flip_weight(nc, pool, psum, identity, raw):
    words = raw[:].bitcast(F32).rearrange("m (p u) -> m u p", u=PAIR)
    flipped = psum.tile([P, PAIR, P], F32, tag="bank")
    for u in range(PAIR):
        nc.tensor.transpose(flipped[:, u, :], words[:, u, :], identity[:])
    w_grouped = pool.tile([P, P * WORD], BF16, align_bytes=MX_ALIGN)
    nc.scalar.copy(
        out=w_grouped[:].bitcast(F32).rearrange("p (col u) -> p col u", u=PAIR),
        in_=flipped[:].rearrange("p u col -> p col u"),
    )
    return w_grouped


def regroup_x(nc, pool, x_raw):
    x_grouped = pool.tile([P, Q * WORD], BF16, align_bytes=MX_ALIGN)
    nc.vector.tensor_copy(
        out=x_grouped[:].bitcast(F32).rearrange("p (q u) -> p q u", u=PAIR),
        in_=x_raw[:].bitcast(F32).rearrange("p (u q) -> p q u", u=PAIR),
    )
    return x_grouped


def quantise(nc, pool, grouped):
    columns = grouped.shape[1] // WORD
    codes = pool.tile([P, columns], U32, align_bytes=MX_ALIGN)
    scales = pool.tile([P, columns], U8, align_bytes=MX_ALIGN)
    nc.vector.quantize_mx(out=codes[:].bitcast(FP8X4), scales=scales[:], in_=grouped[:])
    return codes, scales


def conv_passes(nc, acc, w_mx, operand_mx):
    codes, scales = operand_mx
    for half in range(PAIR):
        w_codes, w_scales = w_mx[half]
        nc.tensor.matmul_mx(
            out=acc[:, half, :],
            lhsT=w_codes[:].bitcast(FP8X4),
            lhsT_scale=w_scales[:],
            rhs=codes[:].bitcast(FP8X4),
            rhs_scale=scales[:],
            start=True,
            stop=True,
        )


def warm_up(nc, scratch, zeros, count):
    for i in range(count):
        nc.tensor.matmul(scratch[:], lhsT=zeros[:], rhs=zeros[:], start=True, stop=True)


def layer1(nc, pool, psum, w_mx, x_mx):
    h_acc = psum.tile([P, PAIR, Q], F32, tag="bank")
    conv_passes(nc, h_acc, w_mx, x_mx)
    h_grouped = pool.tile([P, R * WORD], BF16, align_bytes=MX_ALIGN)
    nc.scalar.activation(
        out=h_grouped[:].rearrange("p (r u k) -> p r u k", u=PAIR, k=TAPS),
        in_=h_acc[:].rearrange("p u (r k) -> p r u k", k=TAPS),
        func=RELU,
        scale=SCALE,
    )
    return h_grouped


def layer2(nc, psum, w_mx, h_mx):
    o_acc = psum.tile([P, PAIR, R], F32, tag="bank")
    conv_passes(nc, o_acc, w_mx, h_mx)
    return o_acc


def finish(nc, pool, o_acc, out_b, on_vector):
    o_sb = pool.tile([P, PAIR, R], F32)
    if on_vector:
        nc.vector.tensor_scalar(out=o_sb[:], in0=o_acc[:], scalar1=SCALE, scalar2=0.0, op0=ALU.mult, op1=ALU.max)
    else:
        nc.scalar.activation(out=o_sb[:], in_=o_acc[:], func=RELU, scale=SCALE)
    queue = nc.sync if on_vector else nc.scalar
    queue.dma_start(out=out_b.rearrange("(m half) r -> m half r", half=PAIR), in_=o_sb[:])


def tile_cnn_pa_s_kernel(tc, x, w0, w1, out):
    nc = tc.nc
    with ExitStack() as ctx:
        consts = ctx.enter_context(tc.tile_pool(name="consts", bufs=1))
        weights = ctx.enter_context(tc.tile_pool(name="weights", bufs=LAYERS * PAIR))
        xs = ctx.enter_context(tc.tile_pool(name="xs", bufs=BATCH))
        hs = ctx.enter_context(tc.tile_pool(name="hs", bufs=BATCH))
        outs = ctx.enter_context(tc.tile_pool(name="outs", bufs=BATCH))
        psum = ctx.enter_context(tc.psum_pool(name="psum", bufs=PSUM_BANKS))
        ctx.enter_context(tc.manual_schedule())

        w0_raw = load_weight(nc, weights, w0)
        x_raw = [load_x(nc, xs, x[0])]
        w1_raw = load_weight(nc, weights, w1)
        x_raw.extend([load_x(nc, xs, x[b]) for b in range(1, BATCH)])

        zeros = consts.tile([P, P], F32)
        nc.vector.memset(zeros[:], 0.0)
        warm = consts.tile([P, 1], F32)
        nc.vector.memset(warm[:], 0.0)
        nc.scalar.activation(out=warm[:], in_=warm[:], func=RELU)
        identity = consts.tile([P, P], F32)
        make_identity(nc, identity[:])

        scratch = psum.tile([P, P], F32, tag="bank")
        warm_up(nc, scratch, zeros, WARM_UPS)
        w0_grouped = [flip_weight(nc, weights, psum, identity, raw) for raw in w0_raw]
        warm_up(nc, scratch, zeros, 2)
        w1_grouped = [flip_weight(nc, weights, psum, identity, raw) for raw in w1_raw]

        x_grouped = [regroup_x(nc, xs, x_raw[0])]
        w0_mx = [quantise(nc, weights, w0_grouped[0])]
        x_mx = quantise(nc, xs, x_grouped[0])
        w0_mx.append(quantise(nc, weights, w0_grouped[1]))
        x_grouped.append(regroup_x(nc, xs, x_raw[1]))
        h_grouped = [layer1(nc, hs, psum, w0_mx, x_mx)]
        for b in range(1, BATCH):
            if b + 1 < BATCH:
                x_grouped.append(regroup_x(nc, xs, x_raw[b + 1]))
            x_mx = quantise(nc, xs, x_grouped[b])
            h_grouped.append(layer1(nc, hs, psum, w0_mx, x_mx))

        w1_mx = [quantise(nc, weights, grouped) for grouped in w1_grouped]
        o_acc = []
        for b in range(BATCH):
            h_mx = quantise(nc, hs, h_grouped[b])
            o_acc.append(layer2(nc, psum, w1_mx, h_mx))
            if b == 2 or b == 3:
                finish(nc, outs, o_acc[b - 2], out[b - 2], True)
        for b in range(2, BATCH):
            finish(nc, outs, o_acc[b], out[b], b == 3)
